import numpy as np
import ml_dtypes


def mxq(x, axis, fmt="e4m3"):
    dtype, down = {"e4m3": (ml_dtypes.float8_e4m3fn, 7), "e5m2": (ml_dtypes.float8_e5m2, 14)}[fmt]
    v = np.moveaxis(np.asarray(x, np.float32).astype(ml_dtypes.bfloat16).astype(np.float64), axis, -1)
    blocks = v.reshape(v.shape[:-1] + (-1, 32))
    amax = np.abs(blocks).max(-1, keepdims=True)
    byte = np.maximum(np.where(amax > 0, np.frexp(amax)[1] - 1 + 127, 0) - down, 1)
    scale = np.exp2(byte - 127.0)
    codes = (blocks / scale).astype(np.float32).astype(dtype).astype(np.float64)
    return np.moveaxis((codes * scale).reshape(v.shape), -1, axis)


WIDE = False


def mx_kscale(k):
    if not WIDE:
        return np.ones(k)
    levels = np.array([10, -10, 5, -5, 0])
    if k % 512:
        return np.exp2(np.random.permutation(np.resize(levels, k // 32))).repeat(32)
    a = np.empty((k // 512, 16))
    for p in range(k // 512):
        a[p, :8] = np.random.permutation(np.resize(levels, 8))
        for g in range(8):
            far = levels[np.abs(levels - a[p, g]) >= 10]
            a[p, g + 8] = far[np.random.randint(len(far))]
    return np.exp2(a.ravel()).repeat(32)


BF16 = ml_dtypes.bfloat16


def bf(x):
    return np.asarray(x, np.float32).astype(BF16)


def f64(x):
    return np.asarray(x).astype(np.float64)


B, T, FS, H, HD = 1, 1024, 512, 12, 128
D = H * HD
EPS = 1e-6
ROPE_BASE = 10000.0


def rmsnorm(u, g):
    var = np.mean(u * u, axis=-1, keepdims=True)
    return u * (1.0 / np.sqrt(var + EPS)) * g


def rope(u, cos, sin):
    ur = u.reshape(B, T, H, HD // 2, 2)
    a, b = ur[..., 0], ur[..., 1]
    c = cos[None, :, None, :]
    s = sin[None, :, None, :]
    return np.stack([a * c - b * s, a * s + b * c], axis=-1).reshape(B, T, H, HD)


def setup_inputs():
    s = mx_kscale(D)
    inv = ROPE_BASE ** (-np.arange(HD // 2) / (HD // 2))
    ang = np.arange(T)[:, None] * inv[None, :]
    return {"x": bf(np.random.standard_normal((B, T, D)) * s),
            "w": bf(np.random.standard_normal((D, D)) / np.sqrt(D) / s[:, None]),
            "b": bf(np.random.standard_normal(D) * 0.1),
            "g": bf(1.0 + 0.1 * np.random.standard_normal(D)),
            "freqs_cos": bf(np.cos(ang)),
            "freqs_sin": bf(np.sin(ang))}


def core(x, w, b, g, freqs_cos, freqs_sin):
    u = (mxq(f64(x), 2, "e4m3") @ mxq(f64(w), 0, "e4m3")) + f64(b)
    return rope(rmsnorm(u, f64(g)).reshape(B, T, H, HD), f64(freqs_cos), f64(freqs_sin))


def e4m3fn_bytes(y):
    return np.clip(np.asarray(y, np.float64), -448.0, 448.0).astype(np.float32).astype(ml_dtypes.float8_e4m3fn).view(np.uint8)


def reference(x, w, b, g, freqs_cos, freqs_sin):
    out = core(x, w, b, g, freqs_cos, freqs_sin)
    s = np.max(np.abs(out), axis=-1, keepdims=True) / 448.0
    return out, e4m3fn_bytes(out / s)

@@ -1,0 +1,439 @@
+from contextlib import ExitStack
+
+import concourse.mybir as mybir
+from concourse.masks import make_identity
+
+F32 = mybir.dt.float32
+BF16 = mybir.dt.bfloat16
+U32 = mybir.dt.uint32
+U8 = mybir.dt.uint8
+FP8X4 = mybir.dt.float8_e4m3fn_x4
+FP8 = mybir.dt.float8_e4m3fn
+ACT = mybir.ActivationFunctionType
+ALU = mybir.AluOpType
+AX = mybir.AxisListType
+
+T, D, H, HD = 1024, 1536, 12, 128
+EPS = 1e-6
+FLOPS = 2 * T * D * D
+
+P = 128
+KP = D // 512
+NB = 256
+NBLK = T // NB
+TPB = NB // P
+WC = 512
+NWC = D // WC
+W_BUFS = 5
+HPS = 3
+SLOTS = H // HPS
+S_UNITS = (4, 6, 7)
+V_CASTS = (1, 2, 4, 5, 7, 8, 10, 11)
+
+
+def tile_causalwanmodel_pa_kernel(tc, x, w, b, g, freqs_cos, freqs_sin, out_0, out_1):
+    nc = tc.nc
+    xv = x.rearrange("o t d -> (o t) d")
+    wv = w.rearrange("(k p j) n -> k p j n", p=P, j=4)
+    o0v = out_0.rearrange("o t h c -> (o t) (h c)")
+    o1v = out_1.rearrange("o t h c -> (o t) (h c)")
+
+    with ExitStack() as ctx:
+        const = ctx.enter_context(tc.tile_pool(name="const", bufs=1))
+        xin = ctx.enter_context(tc.tile_pool(name="xin", bufs=T // P))
+        xgp = ctx.enter_context(tc.tile_pool(name="xgp", bufs=3))
+        wraw = ctx.enter_context(tc.tile_pool(name="wraw", bufs=W_BUFS))
+        wgrp = ctx.enter_context(tc.tile_pool(name="wgrp", bufs=2))
+        up = ctx.enter_context(tc.tile_pool(name="up", bufs=10))
+        yp = ctx.enter_context(tc.tile_pool(name="yp", bufs=2 * H))
+        sqp = ctx.enter_context(tc.tile_pool(name="sqp", bufs=H + 6))
+        op = ctx.enter_context(tc.tile_pool(name="op", bufs=3))
+        small = ctx.enter_context(tc.tile_pool(name="small", bufs=4))
+        ps_mx = ctx.enter_context(tc.psum_pool(name="ps_mx", bufs=3))
+        ps_t = ctx.enter_context(tc.psum_pool(name="ps_t", bufs=4))
+        ps_s = ctx.enter_context(tc.psum_pool(name="ps_s", bufs=1))
+        ctx.enter_context(tc.manual_schedule(engines={mybir.EngineType.PE}))
+
+        cs_raw = const.tile([P, 2, T // P, HD // 2], BF16, name="cs_raw")
+        nc.scalar.dma_start(out=cs_raw[:, 0], in_=freqs_cos.rearrange("(i p) j -> p i j", p=P))
+        nc.scalar.dma_start(out=cs_raw[:, 1], in_=freqs_sin.rearrange("(i p) j -> p i j", p=P))
+        bg_raw = const.tile([P, P], BF16, name="bg_raw")
+        nc.vector.memset(bg_raw[:], 0.0)
+        nc.sync.dma_start(out=bg_raw[0:H, :], in_=b.rearrange("(h c) -> h c", c=HD))
+        nc.sync.dma_start(out=bg_raw[H : 2 * H, :], in_=g.rearrange("(h c) -> h c", c=HD))
+
+        x_sb = {}
+
+        def load_x(i):
+            t = xin.tile([P, D], BF16, name="x_sb", tag="x_sb")
+            nc.sync.dma_start(out=t[:], in_=xv[i * P : (i + 1) * P, :])
+            x_sb[i] = t
+
+        w_raw = {}
+
+        def load_w(n):
+            c, k = n // KP, n % KP
+            t = wraw.tile([P, 4, WC], BF16, name="w_raw", tag="w_raw")
+            nc.sync.dma_start(out=t[:], in_=wv[k, :, :, c * WC : (c + 1) * WC])
+            w_raw[n] = t
+
+        load_w(0)
+        load_w(1)
+        load_x(0)
+        load_x(1)
+        for n in range(2, NWC * KP):
+            load_w(n)
+        for i in range(2, T // P):
+            load_x(i)
+
+        warm = const.tile([P, 1], F32, name="warm")
+        nc.vector.memset(warm[:], 1.0)
+        nc.scalar.activation(out=warm[:], in_=warm[:], func=ACT.Sqrt)
+        zeros = const.tile([P, 1], F32, name="zeros")
+        nc.vector.memset(zeros[:], 0.0)
+        ident = const.tile([P, P], F32, name="ident")
+        make_identity(nc, ident[:])
+        swp = const.tile([P, P], F32, name="swp")
+        iv = ident[:].rearrange("p (j e) -> p j e", e=2)
+        sv = swp[:].rearrange("p (j e) -> p j e", e=2)
+        pat = const.tile([P, HD // 2, 2], F32, name="pat")
+        nc.vector.memset(pat[:, :, 0:1], 1.0)
+        nc.vector.memset(pat[:, :, 1:2], -1.0)
+        nc.vector.tensor_copy(out=sv[:, :, 0:1], in_=iv[:, :, 1:2])
+        nc.vector.tensor_copy(out=sv[:, :, 1:2], in_=iv[:, :, 0:1])
+
+        bg_f = const.tile([P, P], F32, name="bg_f")
+        nc.vector.tensor_copy(out=bg_f[:], in_=bg_raw[:])
+        cols = const.tile([P, 2 * H + 1], F32, name="cols")
+        sgn = const.tile([P, 1], F32, name="sgn")
+
+        def cols_T():
+            cols_ps = ps_t.tile([P, 512], F32, name="tp", tag="tp")
+            nc.tensor.transpose(cols_ps[:, 0:P], bg_f[:], ident[:])
+            nc.tensor.transpose(cols_ps[:, P : 2 * P], pat[:].rearrange("p j e -> p (j e)"), ident[:])
+            nc.scalar.copy(out=cols[:], in_=cols_ps[:, 0 : 2 * H + 1])
+            nc.scalar.copy(out=sgn[:], in_=cols_ps[:, P : P + 1])
+
+        dup = const.tile([P, 2, T // P, HD], F32, name="dup")
+        for s in range(2):
+            nc.scalar.activation(
+                out=dup[:, s].rearrange("p i (j e) -> p (i j) e", e=2),
+                in_=cs_raw[:, s].rearrange("p i j -> p (i j)").unsqueeze(2).to_broadcast([P, T // 2, 2]),
+                func=ACT.Copy,
+            )
+        rotT = const.tile([P, 2, T], F32, name="rotT")
+
+        def rot_T(s, half):
+            tp = ps_t.tile([P, 512], F32, name="tp", tag="tp")
+            for q in range(4):
+                nc.tensor.transpose(tp[:, q * P : (q + 1) * P], dup[:, s, half * 4 + q, :], ident[:])
+            if s == 0:
+                nc.scalar.copy(out=rotT[:, s, half * 512 : (half + 1) * 512], in_=tp[:])
+            else:
+                nc.scalar.activation(
+                    out=rotT[:, s, half * 512 : (half + 1) * 512], in_=tp[:], func=ACT.Copy, scale=sgn[:, 0:1]
+                )
+
+        xq = const.tile([P, KP, T], U32, name="xq", align_bytes=64)
+        xs = const.tile([P, KP, T], U8, name="xs", align_bytes=64)
+        wq = const.tile([P, KP, D], U32, name="wq", align_bytes=64)
+        ws = const.tile([P, KP, D], U8, name="ws", align_bytes=64)
+
+        xts = {}
+        xgs = {}
+
+        def x_T(bk):
+            for k in range(KP):
+                xt = ps_t.tile([P, 2, NB], F32, name="tp", tag="tp")
+                for ii in range(TPB):
+                    words = x_sb[bk * TPB + ii][:].bitcast(F32)
+                    for u in range(2):
+                        nc.tensor.transpose(
+                            xt[:, u, ii * P : (ii + 1) * P], words[:, 256 * k + u : 256 * (k + 1) : 2], ident[:]
+                        )
+                xts[(bk, k)] = xt
+
+        def x_cp(bk, k):
+            xg = xgp.tile([P, 4 * NB], BF16, name="xg", tag="xg", align_bytes=64)
+            nc.scalar.copy(
+                out=xg[:].bitcast(F32).rearrange("p (r u) -> p r u", u=2),
+                in_=xts[(bk, k)][:].rearrange("p u r -> p r u"),
+            )
+            xgs[(bk, k)] = xg
+
+        def x_q(bk, k):
+            t0 = bk * NB
+            nc.vector.quantize_mx(
+                out=xq[:, k, t0 : t0 + NB].bitcast(FP8X4), scales=xs[:, k, t0 : t0 + NB], in_=xgs[(bk, k)][:]
+            )
+
+        wgs = {}
+
+        def w_il(n):
+            tag = "wg_s" if n in S_UNITS else "wg_v"
+            wg = wgrp.tile([P, 4 * WC], BF16, name=tag, tag=tag, align_bytes=64)
+            dst = wg[:].rearrange("p (c i t) -> p c t i", i=4, t=4)
+            src = w_raw[n][:].rearrange("p t (c i) -> p c t i", i=4)
+            if n in S_UNITS:
+                nc.scalar.copy(out=dst, in_=src)
+            else:
+                nc.vector.tensor_copy(out=dst, in_=src)
+            wgs[n] = wg
+
+        def w_q(n):
+            c, k = n // KP, n % KP
+            nc.vector.quantize_mx(
+                out=wq[:, k, c * WC : (c + 1) * WC].bitcast(FP8X4), scales=ws[:, k, c * WC : (c + 1) * WC], in_=wgs[n][:]
+            )
+
+        mxs = {}
+        us = {}
+        sqs = {}
+        ys = {}
+
+        def mx_(bk, h):
+            t0 = bk * NB
+            if h % 2 == 0:
+                mxs[(bk, h // 2)] = ps_mx.tile([P, 2, NB], F32, name="mx", tag="mx")
+            for k in range(KP):
+                nc.tensor.matmul_mx(
+                    out=mxs[(bk, h // 2)][:, h % 2, :],
+                    lhsT=wq[:, k, h * HD : (h + 1) * HD].bitcast(FP8X4),
+                    lhsT_scale=ws[:, k, h * HD : (h + 1) * HD],
+                    rhs=xq[:, k, t0 : t0 + NB].bitcast(FP8X4),
+                    rhs_scale=xs[:, k, t0 : t0 + NB],
+                    start=(k == 0),
+                    stop=(k == KP - 1),
+                )
+
+        def usq(bk, h):
+            mx = mxs[(bk, h // 2)][:, h % 2, :]
+            u = up.tile([P, NB], F32, name="u", tag="u")
+            nc.scalar.activation(out=u[:], in_=mx, func=ACT.Identity, bias=cols[:, h : h + 1], scale=1.0)
+            sq = sqp.tile([P, NB], F32, name="sq", tag="sq")
+            nc.scalar.activation(out=sq[:], in_=mx, func=ACT.Square, bias=cols[:, h : h + 1], scale=1.0)
+            us[(bk, h)] = u
+            sqs[(bk, h)] = sq
+
+        def yy(bk, h):
+            t0 = bk * NB
+            y = yp.tile([P, 2, NB], F32, name="y", tag="y")
+            nc.vector.scalar_tensor_tensor(
+                out=y[:],
+                in0=us[(bk, h)][:].unsqueeze(1).to_broadcast([P, 2, NB]),
+                scalar=cols[:, H + h : H + h + 1],
+                in1=rotT[:, :, t0 : t0 + NB],
+                op0=ALU.mult,
+                op1=ALU.mult,
+            )
+            ys[(bk, h)] = y
+
+        nrm = {}
+
+        def sq_T(bk):
+            ssq_ps = ps_s.tile([P, TPB, P], F32, name="ssq_ps", tag="ssq_ps")
+            for ii in range(TPB):
+                for h in range(H):
+                    nc.tensor.matmul(
+                        out=ssq_ps[:, ii, :],
+                        lhsT=sqs[(bk, h)][:, ii * P : (ii + 1) * P],
+                        rhs=ident[:],
+                        is_transpose=True,
+                        start=(h == 0),
+                        stop=(h == H - 1),
+                    )
+            nrm[bk] = ssq_ps
+
+        def red(bk):
+            ssq = small.tile([P, TPB], F32, name="ssq", tag="ssq")
+            nc.vector.tensor_reduce(out=ssq[:], in_=nrm[bk][:], axis=AX.X, op=ALU.add)
+            nrm[bk] = ssq
+
+        def sqrt_(bk):
+            std = small.tile([P, TPB], F32, name="std", tag="std")
+            nc.scalar.activation(out=std[:], in_=nrm[bk][:], func=ACT.Sqrt, scale=1.0 / D, bias=EPS)
+            nrm[bk] = std
+
+        def rcp(bk):
+            rstd = small.tile([P, TPB], F32, name="rstd", tag="rstd")
+            nc.vector.reciprocal(out=rstd[:], in_=nrm[bk][:])
+            nrm[bk] = rstd
+
+        ops = {}
+        osb = {}
+        facs = {}
+        f8s = {}
+
+        def o_T(bk, ii):
+            for q in range(3):
+                o_ps = ps_t.tile([P, 512], F32, name="tp", tag="tp")
+                for hh in range(4):
+                    y = ys[(bk, 4 * q + hh)]
+                    for s in range(2):
+                        nc.tensor.matmul(
+                            out=o_ps[:, hh * P : (hh + 1) * P],
+                            lhsT=y[:, s, ii * P : (ii + 1) * P],
+                            rhs=(ident[:] if s == 0 else swp[:]),
+                            is_transpose=True,
+                            start=(s == 0),
+                            stop=(s == 1),
+                        )
+                ops[(bk, ii, q)] = o_ps
+
+        def evac(bk, ii, q, on_vector=False):
+            if q == 0:
+                osb[(bk, ii)] = op.tile([P, D], F32, name="o_sb", tag="o_sb")
+            dst = osb[(bk, ii)][:, q * 512 : (q + 1) * 512]
+            if on_vector:
+                nc.vector.tensor_scalar(
+                    out=dst, in0=ops[(bk, ii, q)][:], scalar1=nrm[bk][:, ii : ii + 1], scalar2=None, op0=ALU.mult
+                )
+            else:
+                nc.scalar.activation(out=dst, in_=ops[(bk, ii, q)][:], func=ACT.Copy, scale=nrm[bk][:, ii : ii + 1])
+            if q == 2:
+                rows = slice((bk * TPB + ii) * P, (bk * TPB + ii + 1) * P)
+                nc.sync.dma_start(out=o0v[rows, :], in_=osb[(bk, ii)][:])
+
+        def amax_(bk, ii):
+            amax = small.tile([P, H], F32, name="amax", tag="amax")
+            nc.vector.tensor_reduce(
+                out=amax[:],
+                in_=osb[(bk, ii)][:].rearrange("p (h c) -> p h c", c=HD),
+                axis=AX.X,
+                op=ALU.max,
+                apply_absolute_value=True,
+            )
+            rinv = small.tile([P, H], F32, name="rinv", tag="rinv")
+            nc.vector.reciprocal(out=rinv[:], in_=amax[:])
+            fac = small.tile([P, H], F32, name="fac", tag="fac")
+            nc.vector.tensor_scalar(out=fac[:], in0=rinv[:], scalar1=448.0, scalar2=None, op0=ALU.mult)
+            facs[(bk, ii)] = fac
+            f8s[(bk, ii)] = op.tile([P, D], FP8, name="f8", tag="f8")
+
+        def cast(bk, ii, h):
+            cs = slice(h * HD, (h + 1) * HD)
+            o_sb, fac, f8 = osb[(bk, ii)], facs[(bk, ii)], f8s[(bk, ii)]
+            if h in V_CASTS:
+                nc.vector.tensor_scalar(
+                    out=f8[:, cs], in0=o_sb[:, cs], scalar1=fac[:, h : h + 1], scalar2=None, op0=ALU.mult, saturate=False
+                )
+            else:
+                nc.scalar.activation(
+                    out=f8[:, cs],
+                    in_=o_sb[:, cs],
+                    func=ACT.Identity,
+                    scale=fac[:, h : h + 1],
+                    bias=zeros[:, 0:1],
+                    saturate=False,
+                )
+
+        def casts(bk, ii):
+            for h in range(H):
+                cast(bk, ii, h)
+            rows = slice((bk * TPB + ii) * P, (bk * TPB + ii + 1) * P)
+            nc.sync.dma_start(out=o1v[rows, :], in_=f8s[(bk, ii)][:].bitcast(U8))
+
+        def ok(bk):
+            return 0 <= bk < NBLK
+
+        w_il(0)
+        w_il(1)
+        w_q(0)
+        w_q(1)
+        x_T(0)
+        cols_T()
+        for k in range(KP):
+            x_cp(0, k)
+        for s in range(2):
+            for half in range(2):
+                rot_T(s, half)
+        w_il(2)
+        for k in range(KP):
+            x_q(0, k)
+        w_q(2)
+        w_il(4)
+
+        for p in range(NBLK + 2):
+            a, bb, cc = p, p - 1, p - 2
+            if ok(a):
+                for h in (0, 1, 2, 3):
+                    mx_(a, h)
+            if ok(bb):
+                sq_T(bb)
+            if p >= 1 and ok(p + 1):
+                x_T(p + 1)
+            if ok(cc):
+                for q in range(3):
+                    evac(cc, 1, q)
+            if ok(a):
+                for h in (0, 1, 2, 3):
+                    usq(a, h)
+            if p == 0:
+                w_il(3)
+                w_il(5)
+                w_q(3)
+                w_q(4)
+                w_q(5)
+                w_il(6)
+                w_il(7)
+            if ok(bb):
+                for h in (8, 9, 10, 11):
+                    yy(bb, h)
+            if ok(cc):
+                amax_(cc, 0)
+            if ok(bb):
+                red(bb)
+            if ok(a):
+                for h in (4, 5, 6, 7):
+                    mx_(a, h)
+            if ok(bb):
+                o_T(bb, 0)
+            if p == 0:
+                x_T(1)
+            if ok(a):
+                usq(a, 4)
+                usq(a, 5)
+            if ok(bb):
+                sqrt_(bb)
+            if ok(a):
+                usq(a, 6)
+                usq(a, 7)
+            if ok(p + 1):
+                for k in range(KP):
+                    x_cp(p + 1, k)
+            if ok(a):
+                yy(a, 0)
+                yy(a, 1)
+            if ok(bb):
+                rcp(bb)
+            if ok(a):
+                yy(a, 2)
+                yy(a, 3)
+            if p == 0:
+                w_il(8)
+                w_q(6)
+                w_q(7)
+                w_q(8)
+            if ok(cc):
+                amax_(cc, 1)
+                casts(cc, 0)
+            if ok(a):
+                for h in (8, 9, 10, 11):
+                    mx_(a, h)
+            if ok(bb):
+                o_T(bb, 1)
+            if ok(a):
+                usq(a, 8)
+            if ok(bb):
+                for q in range(3):
+                    evac(bb, 0, q)
+            if ok(a):
+                for h in (9, 10, 11):
+                    usq(a, h)
+                for h in (4, 5, 6, 7):
+                    yy(a, h)
+            if ok(p + 1):
+                for k in range(KP):
+                    x_q(p + 1, k)
+            if ok(cc):
+                casts(cc, 1)

@@ -88,7 +88,7 @@ def tile_causalwanmodel_pa_kernel(tc, x, w, b, g, freqs_cos, freqs_sin, out_0, o
 
         warm = const.tile([P, 1], F32, name="warm")
         nc.vector.memset(warm[:], 1.0)
-        nc.scalar.activation(out=warm[:], in_=warm[:], func=ACT.Sqrt)
+        nc.scalar.activation(out=warm[:], in_=warm[:], func=ACT.Abs_reciprocal_sqrt)
         zeros = const.tile([P, 1], F32, name="zeros")
         nc.vector.memset(zeros[:], 0.0)
         ident = const.tile([P, P], F32, name="ident")
@@ -250,13 +250,8 @@ def tile_causalwanmodel_pa_kernel(tc, x, w, b, g, freqs_cos, freqs_sin, out_0, o
             nrm[bk] = ssq
 
         def sqrt_(bk):
-            std = small.tile([P, TPB], F32, name="std", tag="std")
-            nc.scalar.activation(out=std[:], in_=nrm[bk][:], func=ACT.Sqrt, scale=1.0 / D, bias=EPS)
-            nrm[bk] = std
-
-        def rcp(bk):
             rstd = small.tile([P, TPB], F32, name="rstd", tag="rstd")
-            nc.vector.reciprocal(out=rstd[:], in_=nrm[bk][:])
+            nc.scalar.activation(out=rstd[:], in_=nrm[bk][:], func=ACT.Abs_reciprocal_sqrt, scale=1.0 / D, bias=EPS)
             nrm[bk] = rstd
 
         ops = {}
@@ -404,8 +399,6 @@ def tile_causalwanmodel_pa_kernel(tc, x, w, b, g, freqs_cos, freqs_sin, out_0, o
             if ok(a):
                 yy(a, 0)
                 yy(a, 1)
-            if ok(bb):
-                rcp(bb)
             if ok(a):
                 yy(a, 2)
                 yy(a, 3)

@@ -27,7 +27,7 @@ NWC = D // WC
 W_BUFS = 5
 HPS = 3
 SLOTS = H // HPS
-S_UNITS = (4, 6, 7)
+S_UNITS = (4, 6)
 V_CASTS = (1, 2, 4, 5, 7, 8, 10, 11)
 
 
@@ -50,8 +50,7 @@ def tile_causalwanmodel_pa_kernel(tc, x, w, b, g, freqs_cos, freqs_sin, out_0, o
         op = ctx.enter_context(tc.tile_pool(name="op", bufs=3))
         small = ctx.enter_context(tc.tile_pool(name="small", bufs=4))
         ps_mx = ctx.enter_context(tc.psum_pool(name="ps_mx", bufs=3))
-        ps_t = ctx.enter_context(tc.psum_pool(name="ps_t", bufs=4))
-        ps_s = ctx.enter_context(tc.psum_pool(name="ps_s", bufs=1))
+        ps_t = ctx.enter_context(tc.psum_pool(name="ps_t", bufs=5))
         ctx.enter_context(tc.manual_schedule(engines={mybir.EngineType.PE}))
 
         cs_raw = const.tile([P, 2, T // P, HD // 2], BF16, name="cs_raw")
@@ -231,7 +230,7 @@ def tile_causalwanmodel_pa_kernel(tc, x, w, b, g, freqs_cos, freqs_sin, out_0, o
         nrm = {}
 
         def sq_T(bk):
-            ssq_ps = ps_s.tile([P, TPB, P], F32, name="ssq_ps", tag="ssq_ps")
+            ssq_ps = ps_t.tile([P, TPB, P], F32, name="tp", tag="tp")
             for ii in range(TPB):
                 for h in range(H):
                     nc.tensor.matmul(
@@ -285,23 +284,29 @@ def tile_causalwanmodel_pa_kernel(tc, x, w, b, g, freqs_cos, freqs_sin, out_0, o
                 )
             else:
                 nc.scalar.activation(out=dst, in_=ops[(bk, ii, q)][:], func=ACT.Copy, scale=nrm[bk][:, ii : ii + 1])
-            if q == 2:
-                rows = slice((bk * TPB + ii) * P, (bk * TPB + ii + 1) * P)
+            rows = slice((bk * TPB + ii) * P, (bk * TPB + ii + 1) * P)
+            if bk == NBLK - 1:
+                nc.sync.dma_start(out=o0v[rows, q * 512 : (q + 1) * 512], in_=dst)
+            elif q == 2:
                 nc.sync.dma_start(out=o0v[rows, :], in_=osb[(bk, ii)][:])
 
         def amax_(bk, ii):
             amax = small.tile([P, H], F32, name="amax", tag="amax")
-            nc.vector.tensor_reduce(
-                out=amax[:],
-                in_=osb[(bk, ii)][:].rearrange("p (h c) -> p h c", c=HD),
-                axis=AX.X,
-                op=ALU.max,
-                apply_absolute_value=True,
-            )
             rinv = small.tile([P, H], F32, name="rinv", tag="rinv")
-            nc.vector.reciprocal(out=rinv[:], in_=amax[:])
             fac = small.tile([P, H], F32, name="fac", tag="fac")
-            nc.vector.tensor_scalar(out=fac[:], in0=rinv[:], scalar1=448.0, scalar2=None, op0=ALU.mult)
+            parts = 3 if bk == NBLK - 1 else 1
+            hp = H // parts
+            for j in range(parts):
+                hs = slice(j * hp, (j + 1) * hp)
+                nc.vector.tensor_reduce(
+                    out=amax[:, hs],
+                    in_=osb[(bk, ii)][:, j * hp * HD : (j + 1) * hp * HD].rearrange("p (h c) -> p h c", c=HD),
+                    axis=AX.X,
+                    op=ALU.max,
+                    apply_absolute_value=True,
+                )
+                nc.vector.reciprocal(out=rinv[:, hs], in_=amax[:, hs])
+                nc.vector.tensor_scalar(out=fac[:, hs], in0=rinv[:, hs], scalar1=448.0, scalar2=None, op0=ALU.mult)
             facs[(bk, ii)] = fac
             f8s[(bk, ii)] = op.tile([P, D], FP8, name="f8", tag="f8")
 
@@ -323,10 +328,14 @@ def tile_causalwanmodel_pa_kernel(tc, x, w, b, g, freqs_cos, freqs_sin, out_0, o
                 )
 
         def casts(bk, ii):
-            for h in range(H):
-                cast(bk, ii, h)
             rows = slice((bk * TPB + ii) * P, (bk * TPB + ii + 1) * P)
-            nc.sync.dma_start(out=o1v[rows, :], in_=f8s[(bk, ii)][:].bitcast(U8))
+            parts = 3 if bk == NBLK - 1 else 1
+            hp = H // parts
+            for j in range(parts):
+                for h in range(j * hp, (j + 1) * hp):
+                    cast(bk, ii, h)
+                cs = slice(j * hp * HD, (j + 1) * hp * HD)
+                nc.sync.dma_start(out=o1v[rows, cs], in_=f8s[(bk, ii)][:, cs].bitcast(U8))
 
         def ok(bk):
             return 0 <= bk < NBLK

@@ -25,10 +25,11 @@ TPB = NB // P
 WC = 512
 NWC = D // WC
 W_BUFS = 5
-HPS = 3
-SLOTS = H // HPS
 S_UNITS = (4, 6)
-V_CASTS = (1, 2, 4, 5, 7, 8, 10, 11)
+VH = (1, 2, 4, 5, 7, 8, 10, 11)
+SH = (0, 3, 6, 9)
+VL = (1, 2, 5, 6, 9, 10)
+LAST = NBLK - 1
 
 
 def tile_causalwanmodel_pa_kernel(tc, x, w, b, g, freqs_cos, freqs_sin, out_0, out_1):
@@ -51,15 +52,32 @@ def tile_causalwanmodel_pa_kernel(tc, x, w, b, g, freqs_cos, freqs_sin, out_0, o
         small = ctx.enter_context(tc.tile_pool(name="small", bufs=4))
         ps_mx = ctx.enter_context(tc.psum_pool(name="ps_mx", bufs=3))
         ps_t = ctx.enter_context(tc.psum_pool(name="ps_t", bufs=5))
-        ctx.enter_context(tc.manual_schedule(engines={mybir.EngineType.PE}))
+        ctx.enter_context(tc.manual_schedule())
 
         cs_raw = const.tile([P, 2, T // P, HD // 2], BF16, name="cs_raw")
-        nc.scalar.dma_start(out=cs_raw[:, 0], in_=freqs_cos.rearrange("(i p) j -> p i j", p=P))
-        nc.scalar.dma_start(out=cs_raw[:, 1], in_=freqs_sin.rearrange("(i p) j -> p i j", p=P))
         bg_raw = const.tile([P, P], BF16, name="bg_raw")
-        nc.vector.memset(bg_raw[:], 0.0)
-        nc.sync.dma_start(out=bg_raw[0:H, :], in_=b.rearrange("(h c) -> h c", c=HD))
-        nc.sync.dma_start(out=bg_raw[H : 2 * H, :], in_=g.rearrange("(h c) -> h c", c=HD))
+        warm = const.tile([P, 1], F32, name="warm")
+        zeros = const.tile([P, 1], F32, name="zeros")
+        ident = const.tile([P, P], F32, name="ident")
+        swp = const.tile([P, P], F32, name="swp")
+        pat = const.tile([P, HD // 2, 2], F32, name="pat")
+        bg_f = const.tile([P, P], F32, name="bg_f")
+        cols = const.tile([P, 2 * H + 1], F32, name="cols")
+        sgn = const.tile([P, 1], F32, name="sgn")
+        dupt = const.tile([P, 2, T // P, HD], F32, name="dup")
+        rotT = const.tile([P, 2, T], F32, name="rotT")
+        xq = const.tile([P, KP, T], U32, name="xq", align_bytes=64)
+        xs = const.tile([P, KP, T], U8, name="xs", align_bytes=64)
+        wq = const.tile([P, KP, D], U32, name="wq", align_bytes=64)
+        ws = const.tile([P, KP, D], U8, name="ws", align_bytes=64)
+
+        def load_cs():
+            nc.scalar.dma_start(out=cs_raw[:, 0], in_=freqs_cos.rearrange("(i p) j -> p i j", p=P))
+            nc.scalar.dma_start(out=cs_raw[:, 1], in_=freqs_sin.rearrange("(i p) j -> p i j", p=P))
+
+        def load_bg():
+            nc.sync.dma_start(out=bg_raw[0:H, :], in_=b.rearrange("(h c) -> h c", c=HD))
+            nc.sync.dma_start(out=bg_raw[H : 2 * H, :], in_=g.rearrange("(h c) -> h c", c=HD))
 
         x_sb = {}
 
@@ -76,67 +94,59 @@ def tile_causalwanmodel_pa_kernel(tc, x, w, b, g, freqs_cos, freqs_sin, out_0, o
             nc.sync.dma_start(out=t[:], in_=wv[k, :, :, c * WC : (c + 1) * WC])
             w_raw[n] = t
 
-        load_w(0)
-        load_w(1)
-        load_x(0)
-        load_x(1)
-        for n in range(2, NWC * KP):
-            load_w(n)
-        for i in range(2, T // P):
-            load_x(i)
+        def consts():
+            nc.vector.memset(bg_raw[:], 0.0)
+            nc.vector.memset(warm[:], 1.0)
+            nc.scalar.activation(out=warm[:], in_=warm[:], func=ACT.Abs_reciprocal_sqrt)
+            nc.vector.memset(zeros[:], 0.0)
+            make_identity(nc, ident[:])
+            iv = ident[:].rearrange("p (j e) -> p j e", e=2)
+            sv = swp[:].rearrange("p (j e) -> p j e", e=2)
+            nc.vector.memset(pat[:, :, 0:1], 1.0)
+            nc.vector.memset(pat[:, :, 1:2], -1.0)
+            nc.vector.tensor_copy(out=sv[:, :, 0:1], in_=iv[:, :, 1:2])
+            nc.vector.tensor_copy(out=sv[:, :, 1:2], in_=iv[:, :, 0:1])
 
-        warm = const.tile([P, 1], F32, name="warm")
-        nc.vector.memset(warm[:], 1.0)
-        nc.scalar.activation(out=warm[:], in_=warm[:], func=ACT.Abs_reciprocal_sqrt)
-        zeros = const.tile([P, 1], F32, name="zeros")
-        nc.vector.memset(zeros[:], 0.0)
-        ident = const.tile([P, P], F32, name="ident")
-        make_identity(nc, ident[:])
-        swp = const.tile([P, P], F32, name="swp")
-        iv = ident[:].rearrange("p (j e) -> p j e", e=2)
-        sv = swp[:].rearrange("p (j e) -> p j e", e=2)
-        pat = const.tile([P, HD // 2, 2], F32, name="pat")
-        nc.vector.memset(pat[:, :, 0:1], 1.0)
-        nc.vector.memset(pat[:, :, 1:2], -1.0)
-        nc.vector.tensor_copy(out=sv[:, :, 0:1], in_=iv[:, :, 1:2])
-        nc.vector.tensor_copy(out=sv[:, :, 1:2], in_=iv[:, :, 0:1])
+        def bgf():
+            nc.vector.tensor_copy(out=bg_f[:], in_=bg_raw[:])
 
-        bg_f = const.tile([P, P], F32, name="bg_f")
-        nc.vector.tensor_copy(out=bg_f[:], in_=bg_raw[:])
-        cols = const.tile([P, 2 * H + 1], F32, name="cols")
-        sgn = const.tile([P, 1], F32, name="sgn")
+        cts = {}
+
+        def sgn_T():
+            cts["s"] = ps_t.tile([P, 512], F32, name="tp", tag="tp")
+            nc.tensor.transpose(cts["s"][:, 0:P], pat[:].rearrange("p j e -> p (j e)"), ident[:])
+
+        def sgn_cp():
+            nc.scalar.copy(out=sgn[:], in_=cts["s"][:, 0:1])
 
         def cols_T():
-            cols_ps = ps_t.tile([P, 512], F32, name="tp", tag="tp")
-            nc.tensor.transpose(cols_ps[:, 0:P], bg_f[:], ident[:])
-            nc.tensor.transpose(cols_ps[:, P : 2 * P], pat[:].rearrange("p j e -> p (j e)"), ident[:])
-            nc.scalar.copy(out=cols[:], in_=cols_ps[:, 0 : 2 * H + 1])
-            nc.scalar.copy(out=sgn[:], in_=cols_ps[:, P : P + 1])
+            cts["c"] = ps_t.tile([P, 512], F32, name="tp", tag="tp")
+            nc.tensor.transpose(cts["c"][:, 0:P], bg_f[:], ident[:])
 
-        dup = const.tile([P, 2, T // P, HD], F32, name="dup")
-        for s in range(2):
+        def cols_cp():
+            nc.scalar.copy(out=cols[:], in_=cts["c"][:, 0 : 2 * H + 1])
+
+        def dup(s):
             nc.scalar.activation(
-                out=dup[:, s].rearrange("p i (j e) -> p (i j) e", e=2),
+                out=dupt[:, s].rearrange("p i (j e) -> p (i j) e", e=2),
                 in_=cs_raw[:, s].rearrange("p i j -> p (i j)").unsqueeze(2).to_broadcast([P, T // 2, 2]),
                 func=ACT.Copy,
             )
-        rotT = const.tile([P, 2, T], F32, name="rotT")
+
+        rts = {}
 
         def rot_T(s, half):
             tp = ps_t.tile([P, 512], F32, name="tp", tag="tp")
             for q in range(4):
-                nc.tensor.transpose(tp[:, q * P : (q + 1) * P], dup[:, s, half * 4 + q, :], ident[:])
-            if s == 0:
-                nc.scalar.copy(out=rotT[:, s, half * 512 : (half + 1) * 512], in_=tp[:])
-            else:
-                nc.scalar.activation(
-                    out=rotT[:, s, half * 512 : (half + 1) * 512], in_=tp[:], func=ACT.Copy, scale=sgn[:, 0:1]
-                )
+                nc.tensor.transpose(tp[:, q * P : (q + 1) * P], dupt[:, s, half * 4 + q, :], ident[:])
+            rts[(s, half)] = tp
 
-        xq = const.tile([P, KP, T], U32, name="xq", align_bytes=64)
-        xs = const.tile([P, KP, T], U8, name="xs", align_bytes=64)
-        wq = const.tile([P, KP, D], U32, name="wq", align_bytes=64)
-        ws = const.tile([P, KP, D], U8, name="ws", align_bytes=64)
+        def rot_cp(s, half):
+            dst = rotT[:, s, half * 512 : (half + 1) * 512]
+            if s == 0:
+                nc.scalar.copy(out=dst, in_=rts[(s, half)][:])
+            else:
+                nc.scalar.activation(out=dst, in_=rts[(s, half)][:], func=ACT.Copy, scale=sgn[:, 0:1])
 
         xts = {}
         xgs = {}
@@ -248,72 +258,77 @@ def tile_causalwanmodel_pa_kernel(tc, x, w, b, g, freqs_cos, freqs_sin, out_0, o
             nc.vector.tensor_reduce(out=ssq[:], in_=nrm[bk][:], axis=AX.X, op=ALU.add)
             nrm[bk] = ssq
 
-        def sqrt_(bk):
+        def ars(bk):
             rstd = small.tile([P, TPB], F32, name="rstd", tag="rstd")
             nc.scalar.activation(out=rstd[:], in_=nrm[bk][:], func=ACT.Abs_reciprocal_sqrt, scale=1.0 / D, bias=EPS)
             nrm[bk] = rstd
 
         ops = {}
         osb = {}
+        ams = {}
+        rin = {}
         facs = {}
         f8s = {}
 
-        def o_T(bk, ii):
-            for q in range(3):
-                o_ps = ps_t.tile([P, 512], F32, name="tp", tag="tp")
-                for hh in range(4):
-                    y = ys[(bk, 4 * q + hh)]
-                    for s in range(2):
-                        nc.tensor.matmul(
-                            out=o_ps[:, hh * P : (hh + 1) * P],
-                            lhsT=y[:, s, ii * P : (ii + 1) * P],
-                            rhs=(ident[:] if s == 0 else swp[:]),
-                            is_transpose=True,
-                            start=(s == 0),
-                            stop=(s == 1),
-                        )
-                ops[(bk, ii, q)] = o_ps
+        def rows(bk, ii):
+            return slice((bk * TPB + ii) * P, (bk * TPB + ii + 1) * P)
 
-        def evac(bk, ii, q, on_vector=False):
+        def o_T(bk, ii, q):
+            o_ps = ps_t.tile([P, 512], F32, name="tp", tag="tp")
+            for hh in range(4):
+                y = ys[(bk, 4 * q + hh)]
+                for s in range(2):
+                    nc.tensor.matmul(
+                        out=o_ps[:, hh * P : (hh + 1) * P],
+                        lhsT=y[:, s, ii * P : (ii + 1) * P],
+                        rhs=(ident[:] if s == 0 else swp[:]),
+                        is_transpose=True,
+                        start=(s == 0),
+                        stop=(s == 1),
+                    )
+            ops[(bk, ii, q)] = o_ps
+
+        def evac(bk, ii, q):
             if q == 0:
                 osb[(bk, ii)] = op.tile([P, D], F32, name="o_sb", tag="o_sb")
             dst = osb[(bk, ii)][:, q * 512 : (q + 1) * 512]
-            if on_vector:
-                nc.vector.tensor_scalar(
-                    out=dst, in0=ops[(bk, ii, q)][:], scalar1=nrm[bk][:, ii : ii + 1], scalar2=None, op0=ALU.mult
-                )
-            else:
-                nc.scalar.activation(out=dst, in_=ops[(bk, ii, q)][:], func=ACT.Copy, scale=nrm[bk][:, ii : ii + 1])
-            rows = slice((bk * TPB + ii) * P, (bk * TPB + ii + 1) * P)
-            if bk == NBLK - 1:
-                nc.sync.dma_start(out=o0v[rows, q * 512 : (q + 1) * 512], in_=dst)
-            elif q == 2:
-                nc.sync.dma_start(out=o0v[rows, :], in_=osb[(bk, ii)][:])
+            nc.scalar.activation(out=dst, in_=ops[(bk, ii, q)][:], func=ACT.Copy, scale=nrm[bk][:, ii : ii + 1])
 
-        def amax_(bk, ii):
-            amax = small.tile([P, H], F32, name="amax", tag="amax")
-            rinv = small.tile([P, H], F32, name="rinv", tag="rinv")
-            fac = small.tile([P, H], F32, name="fac", tag="fac")
-            parts = 3 if bk == NBLK - 1 else 1
-            hp = H // parts
-            for j in range(parts):
-                hs = slice(j * hp, (j + 1) * hp)
-                nc.vector.tensor_reduce(
-                    out=amax[:, hs],
-                    in_=osb[(bk, ii)][:, j * hp * HD : (j + 1) * hp * HD].rearrange("p (h c) -> p h c", c=HD),
-                    axis=AX.X,
-                    op=ALU.max,
-                    apply_absolute_value=True,
-                )
-                nc.vector.reciprocal(out=rinv[:, hs], in_=amax[:, hs])
-                nc.vector.tensor_scalar(out=fac[:, hs], in0=rinv[:, hs], scalar1=448.0, scalar2=None, op0=ALU.mult)
-            facs[(bk, ii)] = fac
-            f8s[(bk, ii)] = op.tile([P, D], FP8, name="f8", tag="f8")
+        def part(q, width):
+            return slice(0, 3 * width) if q is None else slice(q * width, (q + 1) * width)
 
-        def cast(bk, ii, h):
+        def st0(bk, ii, q=None):
+            cs = part(q, 512)
+            nc.sync.dma_start(out=o0v[rows(bk, ii), cs], in_=osb[(bk, ii)][:, cs])
+
+        def amax_(bk, ii, q=None):
+            if (bk, ii) not in ams:
+                ams[(bk, ii)] = small.tile([P, H], F32, name="amax", tag="amax")
+                rin[(bk, ii)] = small.tile([P, H], F32, name="rinv", tag="rinv")
+                facs[(bk, ii)] = small.tile([P, H], F32, name="fac", tag="fac")
+                f8s[(bk, ii)] = op.tile([P, D], FP8, name="f8", tag="f8")
+            nc.vector.tensor_reduce(
+                out=ams[(bk, ii)][:, part(q, 4)],
+                in_=osb[(bk, ii)][:, part(q, 512)].rearrange("p (h c) -> p h c", c=HD),
+                axis=AX.X,
+                op=ALU.max,
+                apply_absolute_value=True,
+            )
+
+        def rinv_(bk, ii, q=None):
+            hs = part(q, 4)
+            nc.vector.reciprocal(out=rin[(bk, ii)][:, hs], in_=ams[(bk, ii)][:, hs])
+
+        def fac_(bk, ii, q=None):
+            hs = part(q, 4)
+            nc.vector.tensor_scalar(
+                out=facs[(bk, ii)][:, hs], in0=rin[(bk, ii)][:, hs], scalar1=448.0, scalar2=None, op0=ALU.mult
+            )
+
+        def cast(bk, ii, h, on_vector):
             cs = slice(h * HD, (h + 1) * HD)
             o_sb, fac, f8 = osb[(bk, ii)], facs[(bk, ii)], f8s[(bk, ii)]
-            if h in V_CASTS:
+            if on_vector:
                 nc.vector.tensor_scalar(
                     out=f8[:, cs], in0=o_sb[:, cs], scalar1=fac[:, h : h + 1], scalar2=None, op0=ALU.mult, saturate=False
                 )
@@ -327,115 +342,187 @@ def tile_causalwanmodel_pa_kernel(tc, x, w, b, g, freqs_cos, freqs_sin, out_0, o
                     saturate=False,
                 )
 
-        def casts(bk, ii):
-            rows = slice((bk * TPB + ii) * P, (bk * TPB + ii + 1) * P)
-            parts = 3 if bk == NBLK - 1 else 1
-            hp = H // parts
-            for j in range(parts):
-                for h in range(j * hp, (j + 1) * hp):
-                    cast(bk, ii, h)
-                cs = slice(j * hp * HD, (j + 1) * hp * HD)
-                nc.sync.dma_start(out=o1v[rows, cs], in_=f8s[(bk, ii)][:, cs].bitcast(U8))
+        def st1(bk, ii, q=None):
+            cs = part(q, 512)
+            nc.sync.dma_start(out=o1v[rows(bk, ii), cs], in_=f8s[(bk, ii)][:, cs].bitcast(U8))
 
         def ok(bk):
             return 0 <= bk < NBLK
 
+        def castV(bk, ii, heads):
+            for h in heads:
+                cast(bk, ii, h, True)
+
+        def castS(bk, ii, heads):
+            for h in heads:
+                cast(bk, ii, h, False)
+
+        load_cs()
+        consts()
+        load_w(0)
+        load_w(1)
+        load_x(0)
+        load_x(1)
+        load_w(2)
+        load_bg()
+        for n in (3, 4, 5, 6):
+            load_w(n)
+        load_x(2)
+        load_x(3)
+        load_w(7)
+        load_x(4)
+        load_x(5)
+        load_w(8)
+        load_x(6)
+        load_x(7)
+
+        sgn_T()
+        dup(0)
+        dup(1)
+        sgn_cp()
         w_il(0)
         w_il(1)
         w_q(0)
         w_q(1)
         x_T(0)
-        cols_T()
         for k in range(KP):
             x_cp(0, k)
-        for s in range(2):
-            for half in range(2):
-                rot_T(s, half)
         w_il(2)
         for k in range(KP):
             x_q(0, k)
         w_q(2)
+        w_il(3)
+        for s in range(2):
+            for half in range(2):
+                rot_T(s, half)
+                rot_cp(s, half)
         w_il(4)
+        bgf()
+        cols_T()
+        cols_cp()
+        w_il(5)
+        w_q(3)
 
-        for p in range(NBLK + 2):
+        for p in range(NBLK + 1):
             a, bb, cc = p, p - 1, p - 2
             if ok(a):
                 for h in (0, 1, 2, 3):
                     mx_(a, h)
             if ok(bb):
                 sq_T(bb)
-            if p >= 1 and ok(p + 1):
-                x_T(p + 1)
-            if ok(cc):
-                for q in range(3):
-                    evac(cc, 1, q)
+            if p >= 2 and ok(a + 1):
+                x_T(a + 1)
             if ok(a):
                 for h in (0, 1, 2, 3):
                     usq(a, h)
+            if ok(cc) and cc < LAST:
+                castS(cc, 0, SH)
             if p == 0:
-                w_il(3)
-                w_il(5)
-                w_q(3)
-                w_q(4)
                 w_q(5)
-                w_il(6)
+                w_q(4)
                 w_il(7)
-            if ok(bb):
-                for h in (8, 9, 10, 11):
-                    yy(bb, h)
-            if ok(cc):
-                amax_(cc, 0)
+                w_il(6)
+            if ok(a):
+                for h in (0, 1, 2, 3):
+                    yy(a, h)
+            if ok(cc) and cc < LAST:
+                castV(cc, 0, VH[4:])
+                st1(cc, 0)
             if ok(bb):
                 red(bb)
+            if ok(cc) and cc < LAST:
+                amax_(cc, 1)
+            if p >= 1 and ok(a + 1):
+                for k in range(KP):
+                    x_cp(a + 1, k)
+            if ok(bb):
+                ars(bb)
+            if ok(cc) and cc < LAST:
+                rinv_(cc, 1)
+            if p >= 1 and ok(a + 1):
+                for k in range(KP):
+                    x_q(a + 1, k)
+            if ok(cc) and cc < LAST:
+                fac_(cc, 1)
             if ok(a):
                 for h in (4, 5, 6, 7):
                     mx_(a, h)
-            if ok(bb):
-                o_T(bb, 0)
             if p == 0:
                 x_T(1)
-            if ok(a):
-                usq(a, 4)
-                usq(a, 5)
+                x_T(2)
             if ok(bb):
-                sqrt_(bb)
+                for q in range(3):
+                    o_T(bb, 0, q)
             if ok(a):
-                usq(a, 6)
-                usq(a, 7)
-            if ok(p + 1):
-                for k in range(KP):
-                    x_cp(p + 1, k)
-            if ok(a):
-                yy(a, 0)
-                yy(a, 1)
-            if ok(a):
-                yy(a, 2)
-                yy(a, 3)
+                for h in (4, 5, 6, 7):
+                    usq(a, h)
             if p == 0:
                 w_il(8)
                 w_q(6)
                 w_q(7)
                 w_q(8)
-            if ok(cc):
-                amax_(cc, 1)
-                casts(cc, 0)
+                for k in range(KP):
+                    x_cp(1, k)
+            if ok(bb) and bb < LAST:
+                for q in range(3):
+                    evac(bb, 0, q)
+                st0(bb, 0)
+            if bb == LAST:
+                for q in range(3):
+                    evac(bb, 0, q)
+                    st0(bb, 0, q)
+            if ok(a):
+                for h in (4, 5, 6, 7):
+                    yy(a, h)
+            if ok(cc) and cc < LAST:
+                castV(cc, 1, VH)
+                castS(cc, 1, SH)
+                st1(cc, 1)
+            if p == 0:
+                for k in range(KP):
+                    x_q(1, k)
+            if ok(bb) and bb < LAST:
+                amax_(bb, 0)
             if ok(a):
                 for h in (8, 9, 10, 11):
                     mx_(a, h)
             if ok(bb):
-                o_T(bb, 1)
-            if ok(a):
-                usq(a, 8)
-            if ok(bb):
                 for q in range(3):
-                    evac(bb, 0, q)
+                    o_T(bb, 1, q)
             if ok(a):
-                for h in (9, 10, 11):
+                for h in (8, 9, 10, 11):
                     usq(a, h)
-                for h in (4, 5, 6, 7):
+            if ok(bb) and bb < LAST:
+                for q in range(3):
+                    evac(bb, 1, q)
+                st0(bb, 1)
+            if ok(a):
+                for h in (8, 9):
                     yy(a, h)
-            if ok(p + 1):
-                for k in range(KP):
-                    x_q(p + 1, k)
-            if ok(cc):
-                casts(cc, 1)
+            if ok(bb) and bb < LAST:
+                rinv_(bb, 0)
+            if ok(a):
+                for h in (10, 11):
+                    yy(a, h)
+            if ok(bb) and bb < LAST:
+                fac_(bb, 0)
+                castV(bb, 0, VH[:4])
+            if bb == LAST:
+                units = [(ii, q) for ii in range(TPB) for q in range(3)]
+                for q in range(3):
+                    evac(bb, 1, q)
+                    st0(bb, 1, q)
+                for n in range(len(units) + 2):
+                    if n < len(units):
+                        amax_(bb, units[n][0], units[n][1])
+                    if 1 <= n <= len(units):
+                        rinv_(bb, units[n - 1][0], units[n - 1][1])
+                    if n >= 2:
+                        ii, q = units[n - 2]
+                        castV(bb, ii, [h for h in VL if h // 4 == q])
+                    if 1 <= n <= len(units):
+                        fac_(bb, units[n - 1][0], units[n - 1][1])
+                    if n >= 2:
+                        ii, q = units[n - 2]
+                        castS(bb, ii, [h for h in range(4 * q, 4 * q + 4) if h not in VL])
+                        st1(bb, ii, q)

@@ -437,13 +437,13 @@ def tile_causalwanmodel_pa_kernel(tc, x, w, b, g, freqs_cos, freqs_sin, out_0, o
                     x_cp(a + 1, k)
             if ok(bb):
                 ars(bb)
-            if ok(cc) and cc < LAST:
+            if p >= 1 and ok(a + 1):
+                x_q(a + 1, 0)
+                x_q(a + 1, 1)
+            if ok(cc) and cc < LAST and ok(a + 1):
                 rinv_(cc, 1)
             if p >= 1 and ok(a + 1):
-                for k in range(KP):
-                    x_q(a + 1, k)
-            if ok(cc) and cc < LAST:
-                fac_(cc, 1)
+                x_q(a + 1, 2)
             if ok(a):
                 for h in (4, 5, 6, 7):
                     mx_(a, h)
@@ -472,9 +472,17 @@ def tile_causalwanmodel_pa_kernel(tc, x, w, b, g, freqs_cos, freqs_sin, out_0, o
                     evac(bb, 0, q)
                     st0(bb, 0, q)
             if ok(a):
-                for h in (4, 5, 6, 7):
-                    yy(a, h)
-            if ok(cc) and cc < LAST:
+                yy(a, 4)
+            if ok(cc) and cc < LAST and ok(a) and not ok(a + 1):
+                rinv_(cc, 1)
+            if ok(a):
+                yy(a, 5)
+            if ok(cc) and cc < LAST and ok(a):
+                fac_(cc, 1)
+            if ok(a):
+                yy(a, 6)
+                yy(a, 7)
+            if ok(cc) and cc < LAST and ok(a):
                 castV(cc, 1, VH)
                 castS(cc, 1, SH)
                 st1(cc, 1)
@@ -497,32 +505,33 @@ def tile_causalwanmodel_pa_kernel(tc, x, w, b, g, freqs_cos, freqs_sin, out_0, o
                     evac(bb, 1, q)
                 st0(bb, 1)
             if ok(a):
-                for h in (8, 9):
-                    yy(a, h)
+                yy(a, 8)
             if ok(bb) and bb < LAST:
                 rinv_(bb, 0)
             if ok(a):
-                for h in (10, 11):
-                    yy(a, h)
+                yy(a, 9)
             if ok(bb) and bb < LAST:
                 fac_(bb, 0)
+            if ok(a):
+                yy(a, 10)
+                yy(a, 11)
+            if ok(bb) and bb < LAST:
                 castV(bb, 0, VH[:4])
             if bb == LAST:
-                units = [(ii, q) for ii in range(TPB) for q in range(3)]
                 for q in range(3):
                     evac(bb, 1, q)
                     st0(bb, 1, q)
-                for n in range(len(units) + 2):
-                    if n < len(units):
-                        amax_(bb, units[n][0], units[n][1])
-                    if 1 <= n <= len(units):
-                        rinv_(bb, units[n - 1][0], units[n - 1][1])
-                    if n >= 2:
-                        ii, q = units[n - 2]
-                        castV(bb, ii, [h for h in VL if h // 4 == q])
-                    if 1 <= n <= len(units):
-                        fac_(bb, units[n - 1][0], units[n - 1][1])
-                    if n >= 2:
-                        ii, q = units[n - 2]
-                        castS(bb, ii, [h for h in range(4 * q, 4 * q + 4) if h not in VL])
-                        st1(bb, ii, q)
+                units = [(cc, 1, None)] + [(bb, ii, q) for ii in range(TPB) for q in range(3)]
+                for n in range(len(units) + 3):
+                    if 1 <= n < len(units):
+                        amax_(*units[n])
+                    if 0 <= n - 1 < len(units):
+                        rinv_(*units[n - 1])
+                    if 0 <= n - 2 < len(units):
+                        fac_(*units[n - 2])
+                    if 0 <= n - 3 < len(units):
+                        bk, ii, q = units[n - 3]
+                        heads = range(H) if q is None else range(4 * q, 4 * q + 4)
+                        castV(bk, ii, [h for h in heads if h in (VH if q is None else VL)])
+                        castS(bk, ii, [h for h in heads if h not in (VH if q is None else VL)])
+                        st1(bk, ii, q)

@@ -26,8 +26,7 @@ WC = 512
 NWC = D // WC
 W_BUFS = 5
 S_UNITS = (4, 6)
-VH = (1, 2, 4, 5, 7, 8, 10, 11)
-SH = (0, 3, 6, 9)
+VHB = ((1, 2, 3, 4, 5, 7, 8, 9, 10, 11), (1, 2, 3, 4, 5, 7, 8, 9, 10, 11), (1, 2, 5, 7, 8, 10), ())
 VL = (1, 2, 5, 6, 9, 10)
 LAST = NBLK - 1
 
@@ -416,7 +415,7 @@ def tile_causalwanmodel_pa_kernel(tc, x, w, b, g, freqs_cos, freqs_sin, out_0, o
                 for h in (0, 1, 2, 3):
                     usq(a, h)
             if ok(cc) and cc < LAST:
-                castS(cc, 0, SH)
+                castS(cc, 0, [h for h in range(H) if h not in VHB[cc]])
             if p == 0:
                 w_q(5)
                 w_q(4)
@@ -426,7 +425,7 @@ def tile_causalwanmodel_pa_kernel(tc, x, w, b, g, freqs_cos, freqs_sin, out_0, o
                 for h in (0, 1, 2, 3):
                     yy(a, h)
             if ok(cc) and cc < LAST:
-                castV(cc, 0, VH[4:])
+                castV(cc, 0, VHB[cc][4:])
                 st1(cc, 0)
             if ok(bb):
                 red(bb)
@@ -453,6 +452,9 @@ def tile_causalwanmodel_pa_kernel(tc, x, w, b, g, freqs_cos, freqs_sin, out_0, o
             if ok(bb):
                 for q in range(3):
                     o_T(bb, 0, q)
+            if p == 0:
+                for k in range(KP):
+                    x_cp(1, k)
             if ok(a):
                 for h in (4, 5, 6, 7):
                     usq(a, h)
@@ -461,8 +463,6 @@ def tile_causalwanmodel_pa_kernel(tc, x, w, b, g, freqs_cos, freqs_sin, out_0, o
                 w_q(6)
                 w_q(7)
                 w_q(8)
-                for k in range(KP):
-                    x_cp(1, k)
             if ok(bb) and bb < LAST:
                 for q in range(3):
                     evac(bb, 0, q)
@@ -471,6 +471,9 @@ def tile_causalwanmodel_pa_kernel(tc, x, w, b, g, freqs_cos, freqs_sin, out_0, o
                 for q in range(3):
                     evac(bb, 0, q)
                     st0(bb, 0, q)
+            if p == 0:
+                for k in range(KP):
+                    x_q(1, k)
             if ok(a):
                 yy(a, 4)
             if ok(cc) and cc < LAST and ok(a) and not ok(a + 1):
@@ -483,12 +486,9 @@ def tile_causalwanmodel_pa_kernel(tc, x, w, b, g, freqs_cos, freqs_sin, out_0, o
                 yy(a, 6)
                 yy(a, 7)
             if ok(cc) and cc < LAST and ok(a):
-                castV(cc, 1, VH)
-                castS(cc, 1, SH)
+                castV(cc, 1, VHB[cc])
+                castS(cc, 1, [h for h in range(H) if h not in VHB[cc]])
                 st1(cc, 1)
-            if p == 0:
-                for k in range(KP):
-                    x_q(1, k)
             if ok(bb) and bb < LAST:
                 amax_(bb, 0)
             if ok(a):
@@ -516,7 +516,7 @@ def tile_causalwanmodel_pa_kernel(tc, x, w, b, g, freqs_cos, freqs_sin, out_0, o
                 yy(a, 10)
                 yy(a, 11)
             if ok(bb) and bb < LAST:
-                castV(bb, 0, VH[:4])
+                castV(bb, 0, VHB[bb][:4])
             if bb == LAST:
                 for q in range(3):
                     evac(bb, 1, q)
@@ -532,6 +532,6 @@ def tile_causalwanmodel_pa_kernel(tc, x, w, b, g, freqs_cos, freqs_sin, out_0, o
                     if 0 <= n - 3 < len(units):
                         bk, ii, q = units[n - 3]
                         heads = range(H) if q is None else range(4 * q, 4 * q + 4)
-                        castV(bk, ii, [h for h in heads if h in (VH if q is None else VL)])
-                        castS(bk, ii, [h for h in heads if h not in (VH if q is None else VL)])
+                        castV(bk, ii, [h for h in heads if h in (VHB[bk] if q is None else VL)])
+                        castS(bk, ii, [h for h in heads if h not in (VHB[bk] if q is None else VL)])
                         st1(bk, ii, q)

@@ -27,6 +27,7 @@ NWC = D // WC
 W_BUFS = 5
 S_UNITS = (4, 6)
 VHB = ((1, 2, 3, 4, 5, 7, 8, 9, 10, 11), (1, 2, 3, 4, 5, 7, 8, 9, 10, 11), (1, 2, 5, 7, 8, 10), ())
+EARLY = ((0, 0),)
 VL = (1, 2, 5, 6, 9, 10)
 LAST = NBLK - 1
 
@@ -254,7 +255,11 @@ def tile_causalwanmodel_pa_kernel(tc, x, w, b, g, freqs_cos, freqs_sin, out_0, o
 
         def red(bk):
             ssq = small.tile([P, TPB], F32, name="ssq", tag="ssq")
-            nc.vector.tensor_reduce(out=ssq[:], in_=nrm[bk][:], axis=AX.X, op=ALU.add)
+            for ii in range(TPB):
+                junk = small.tile([P, P], F32, name="junk", tag="junk")
+                nc.scalar.activation(
+                    out=junk[:], in_=nrm[bk][:, ii, :], func=ACT.Copy, accum_out=ssq[:, ii : ii + 1]
+                )
             nrm[bk] = ssq
 
         def ars(bk):
@@ -383,6 +388,8 @@ def tile_causalwanmodel_pa_kernel(tc, x, w, b, g, freqs_cos, freqs_sin, out_0, o
         w_il(1)
         w_q(0)
         w_q(1)
+        for s, half in EARLY:
+            rot_T(s, half)
         x_T(0)
         for k in range(KP):
             x_cp(0, k)
@@ -393,7 +400,8 @@ def tile_causalwanmodel_pa_kernel(tc, x, w, b, g, freqs_cos, freqs_sin, out_0, o
         w_il(3)
         for s in range(2):
             for half in range(2):
-                rot_T(s, half)
+                if (s, half) not in EARLY:
+                    rot_T(s, half)
                 rot_cp(s, half)
         w_il(4)
         bgf()

from contextlib import ExitStack

import concourse.mybir as mybir
from concourse.masks import make_identity

F32 = mybir.dt.float32
BF16 = mybir.dt.bfloat16
U32 = mybir.dt.uint32
U8 = mybir.dt.uint8
FP8X4 = mybir.dt.float8_e4m3fn_x4
FP8 = mybir.dt.float8_e4m3fn
ACT = mybir.ActivationFunctionType
ALU = mybir.AluOpType
AX = mybir.AxisListType

T, D, H, HD = 1024, 1536, 12, 128
EPS = 1e-6
FLOPS = 2 * T * D * D

P = 128
KP = D // 512
NB = 256
NBLK = T // NB
TPB = NB // P
WC = 512
NWC = D // WC
W_BUFS = 5
S_UNITS = (4, 6)
VHB = ((1, 2, 3, 4, 5, 7, 8, 9, 10, 11), (1, 2, 3, 4, 5, 7, 8, 9, 10, 11), (1, 2, 5, 7, 8, 10), ())
EARLY = ((0, 0),)
VL = (1, 2, 5, 6, 9, 10)
LAST = NBLK - 1


def tile_causalwanmodel_pa_kernel(tc, x, w, b, g, freqs_cos, freqs_sin, out_0, out_1):
    nc = tc.nc
    xv = x.rearrange("o t d -> (o t) d")
    wv = w.rearrange("(k p j) n -> k p j n", p=P, j=4)
    o0v = out_0.rearrange("o t h c -> (o t) (h c)")
    o1v = out_1.rearrange("o t h c -> (o t) (h c)")

    with ExitStack() as ctx:
        const = ctx.enter_context(tc.tile_pool(name="const", bufs=1))
        xin = ctx.enter_context(tc.tile_pool(name="xin", bufs=T // P))
        xgp = ctx.enter_context(tc.tile_pool(name="xgp", bufs=3))
        wraw = ctx.enter_context(tc.tile_pool(name="wraw", bufs=W_BUFS))
        wgrp = ctx.enter_context(tc.tile_pool(name="wgrp", bufs=2))
        up = ctx.enter_context(tc.tile_pool(name="up", bufs=10))
        yp = ctx.enter_context(tc.tile_pool(name="yp", bufs=2 * H))
        sqp = ctx.enter_context(tc.tile_pool(name="sqp", bufs=H + 6))
        op = ctx.enter_context(tc.tile_pool(name="op", bufs=3))
        small = ctx.enter_context(tc.tile_pool(name="small", bufs=4))
        ps_mx = ctx.enter_context(tc.psum_pool(name="ps_mx", bufs=3))
        ps_t = ctx.enter_context(tc.psum_pool(name="ps_t", bufs=5))
        ctx.enter_context(tc.manual_schedule())

        cs_raw = const.tile([P, 2, T // P, HD // 2], BF16, name="cs_raw")
        bg_raw = const.tile([P, P], BF16, name="bg_raw")
        warm = const.tile([P, 1], F32, name="warm")
        zeros = const.tile([P, 1], F32, name="zeros")
        ident = const.tile([P, P], F32, name="ident")
        swp = const.tile([P, P], F32, name="swp")
        pat = const.tile([P, HD // 2, 2], F32, name="pat")
        bg_f = const.tile([P, P], F32, name="bg_f")
        cols = const.tile([P, 2 * H + 1], F32, name="cols")
        sgn = const.tile([P, 1], F32, name="sgn")
        dupt = const.tile([P, 2, T // P, HD], F32, name="dup")
        rotT = const.tile([P, 2, T], F32, name="rotT")
        xq = const.tile([P, KP, T], U32, name="xq", align_bytes=64)
        xs = const.tile([P, KP, T], U8, name="xs", align_bytes=64)
        wq = const.tile([P, KP, D], U32, name="wq", align_bytes=64)
        ws = const.tile([P, KP, D], U8, name="ws", align_bytes=64)

        def load_cs():
            nc.scalar.dma_start(out=cs_raw[:, 0], in_=freqs_cos.rearrange("(i p) j -> p i j", p=P))
            nc.scalar.dma_start(out=cs_raw[:, 1], in_=freqs_sin.rearrange("(i p) j -> p i j", p=P))

        def load_bg():
            nc.sync.dma_start(out=bg_raw[0:H, :], in_=b.rearrange("(h c) -> h c", c=HD))
            nc.sync.dma_start(out=bg_raw[H : 2 * H, :], in_=g.rearrange("(h c) -> h c", c=HD))

        x_sb = {}

        def load_x(i):
            t = xin.tile([P, D], BF16, name="x_sb", tag="x_sb")
            nc.sync.dma_start(out=t[:], in_=xv[i * P : (i + 1) * P, :])
            x_sb[i] = t

        w_raw = {}

        def load_w(n):
            c, k = n // KP, n % KP
            t = wraw.tile([P, 4, WC], BF16, name="w_raw", tag="w_raw")
            nc.sync.dma_start(out=t[:], in_=wv[k, :, :, c * WC : (c + 1) * WC])
            w_raw[n] = t

        def consts():
            nc.vector.memset(bg_raw[:], 0.0)
            nc.vector.memset(warm[:], 1.0)
            nc.scalar.activation(out=warm[:], in_=warm[:], func=ACT.Abs_reciprocal_sqrt)
            nc.vector.memset(zeros[:], 0.0)
            make_identity(nc, ident[:])
            iv = ident[:].rearrange("p (j e) -> p j e", e=2)
            sv = swp[:].rearrange("p (j e) -> p j e", e=2)
            nc.vector.memset(pat[:, :, 0:1], 1.0)
            nc.vector.memset(pat[:, :, 1:2], -1.0)
            nc.vector.tensor_copy(out=sv[:, :, 0:1], in_=iv[:, :, 1:2])
            nc.vector.tensor_copy(out=sv[:, :, 1:2], in_=iv[:, :, 0:1])

        def bgf():
            nc.vector.tensor_copy(out=bg_f[:], in_=bg_raw[:])

        cts = {}

        def sgn_T():
            cts["s"] = ps_t.tile([P, 512], F32, name="tp", tag="tp")
            nc.tensor.transpose(cts["s"][:, 0:P], pat[:].rearrange("p j e -> p (j e)"), ident[:])

        def sgn_cp():
            nc.scalar.copy(out=sgn[:], in_=cts["s"][:, 0:1])

        def cols_T():
            cts["c"] = ps_t.tile([P, 512], F32, name="tp", tag="tp")
            nc.tensor.transpose(cts["c"][:, 0:P], bg_f[:], ident[:])

        def cols_cp():
            nc.scalar.copy(out=cols[:], in_=cts["c"][:, 0 : 2 * H + 1])

        def dup(s):
            nc.scalar.activation(
                out=dupt[:, s].rearrange("p i (j e) -> p (i j) e", e=2),
                in_=cs_raw[:, s].rearrange("p i j -> p (i j)").unsqueeze(2).to_broadcast([P, T // 2, 2]),
                func=ACT.Copy,
            )

        rts = {}

        def rot_T(s, half):
            tp = ps_t.tile([P, 512], F32, name="tp", tag="tp")
            for q in range(4):
                nc.tensor.transpose(tp[:, q * P : (q + 1) * P], dupt[:, s, half * 4 + q, :], ident[:])
            rts[(s, half)] = tp

        def rot_cp(s, half):
            dst = rotT[:, s, half * 512 : (half + 1) * 512]
            if s == 0:
                nc.scalar.copy(out=dst, in_=rts[(s, half)][:])
            else:
                nc.scalar.activation(out=dst, in_=rts[(s, half)][:], func=ACT.Copy, scale=sgn[:, 0:1])

        xts = {}
        xgs = {}

        def x_T(bk):
            for k in range(KP):
                xt = ps_t.tile([P, 2, NB], F32, name="tp", tag="tp")
                for ii in range(TPB):
                    words = x_sb[bk * TPB + ii][:].bitcast(F32)
                    for u in range(2):
                        nc.tensor.transpose(
                            xt[:, u, ii * P : (ii + 1) * P], words[:, 256 * k + u : 256 * (k + 1) : 2], ident[:]
                        )
                xts[(bk, k)] = xt

        def x_cp(bk, k):
            xg = xgp.tile([P, 4 * NB], BF16, name="xg", tag="xg", align_bytes=64)
            nc.scalar.copy(
                out=xg[:].bitcast(F32).rearrange("p (r u) -> p r u", u=2),
                in_=xts[(bk, k)][:].rearrange("p u r -> p r u"),
            )
            xgs[(bk, k)] = xg

        def x_q(bk, k):
            t0 = bk * NB
            nc.vector.quantize_mx(
                out=xq[:, k, t0 : t0 + NB].bitcast(FP8X4), scales=xs[:, k, t0 : t0 + NB], in_=xgs[(bk, k)][:]
            )

        wgs = {}

        def w_il(n):
            tag = "wg_s" if n in S_UNITS else "wg_v"
            wg = wgrp.tile([P, 4 * WC], BF16, name=tag, tag=tag, align_bytes=64)
            dst = wg[:].rearrange("p (c i t) -> p c t i", i=4, t=4)
            src = w_raw[n][:].rearrange("p t (c i) -> p c t i", i=4)
            if n in S_UNITS:
                nc.scalar.copy(out=dst, in_=src)
            else:
                nc.vector.tensor_copy(out=dst, in_=src)
            wgs[n] = wg

        def w_q(n):
            c, k = n // KP, n % KP
            nc.vector.quantize_mx(
                out=wq[:, k, c * WC : (c + 1) * WC].bitcast(FP8X4), scales=ws[:, k, c * WC : (c + 1) * WC], in_=wgs[n][:]
            )

        mxs = {}
        us = {}
        sqs = {}
        ys = {}

        def mx_(bk, h):
            t0 = bk * NB
            if h % 2 == 0:
                mxs[(bk, h // 2)] = ps_mx.tile([P, 2, NB], F32, name="mx", tag="mx")
            for k in range(KP):
                nc.tensor.matmul_mx(
                    out=mxs[(bk, h // 2)][:, h % 2, :],
                    lhsT=wq[:, k, h * HD : (h + 1) * HD].bitcast(FP8X4),
                    lhsT_scale=ws[:, k, h * HD : (h + 1) * HD],
                    rhs=xq[:, k, t0 : t0 + NB].bitcast(FP8X4),
                    rhs_scale=xs[:, k, t0 : t0 + NB],
                    start=(k == 0),
                    stop=(k == KP - 1),
                )

        def usq(bk, h):
            mx = mxs[(bk, h // 2)][:, h % 2, :]
            u = up.tile([P, NB], F32, name="u", tag="u")
            nc.scalar.activation(out=u[:], in_=mx, func=ACT.Identity, bias=cols[:, h : h + 1], scale=1.0)
            sq = sqp.tile([P, NB], F32, name="sq", tag="sq")
            nc.scalar.activation(out=sq[:], in_=mx, func=ACT.Square, bias=cols[:, h : h + 1], scale=1.0)
            us[(bk, h)] = u
            sqs[(bk, h)] = sq

        def yy(bk, h):
            t0 = bk * NB
            y = yp.tile([P, 2, NB], F32, name="y", tag="y")
            nc.vector.scalar_tensor_tensor(
                out=y[:],
                in0=us[(bk, h)][:].unsqueeze(1).to_broadcast([P, 2, NB]),
                scalar=cols[:, H + h : H + h + 1],
                in1=rotT[:, :, t0 : t0 + NB],
                op0=ALU.mult,
                op1=ALU.mult,
            )
            ys[(bk, h)] = y

        nrm = {}

        def sq_T(bk):
            ssq_ps = ps_t.tile([P, TPB, P], F32, name="tp", tag="tp")
            for ii in range(TPB):
                for h in range(H):
                    nc.tensor.matmul(
                        out=ssq_ps[:, ii, :],
                        lhsT=sqs[(bk, h)][:, ii * P : (ii + 1) * P],
                        rhs=ident[:],
                        is_transpose=True,
                        start=(h == 0),
                        stop=(h == H - 1),
                    )
            nrm[bk] = ssq_ps

        def red(bk):
            ssq = small.tile([P, TPB], F32, name="ssq", tag="ssq")
            for ii in range(TPB):
                junk = small.tile([P, P], F32, name="junk", tag="junk")
                nc.scalar.activation(
                    out=junk[:], in_=nrm[bk][:, ii, :], func=ACT.Copy, accum_out=ssq[:, ii : ii + 1]
                )
            nrm[bk] = ssq

        def ars(bk):
            rstd = small.tile([P, TPB], F32, name="rstd", tag="rstd")
            nc.scalar.activation(out=rstd[:], in_=nrm[bk][:], func=ACT.Abs_reciprocal_sqrt, scale=1.0 / D, bias=EPS)
            nrm[bk] = rstd

        ops = {}
        osb = {}
        ams = {}
        rin = {}
        facs = {}
        f8s = {}

        def rows(bk, ii):
            return slice((bk * TPB + ii) * P, (bk * TPB + ii + 1) * P)

        def o_T(bk, ii, q):
            o_ps = ps_t.tile([P, 512], F32, name="tp", tag="tp")
            for hh in range(4):
                y = ys[(bk, 4 * q + hh)]
                for s in range(2):
                    nc.tensor.matmul(
                        out=o_ps[:, hh * P : (hh + 1) * P],
                        lhsT=y[:, s, ii * P : (ii + 1) * P],
                        rhs=(ident[:] if s == 0 else swp[:]),
                        is_transpose=True,
                        start=(s == 0),
                        stop=(s == 1),
                    )
            ops[(bk, ii, q)] = o_ps

        def evac(bk, ii, q):
            if q == 0:
                osb[(bk, ii)] = op.tile([P, D], F32, name="o_sb", tag="o_sb")
            dst = osb[(bk, ii)][:, q * 512 : (q + 1) * 512]
            nc.scalar.activation(out=dst, in_=ops[(bk, ii, q)][:], func=ACT.Copy, scale=nrm[bk][:, ii : ii + 1])

        def part(q, width):
            return slice(0, 3 * width) if q is None else slice(q * width, (q + 1) * width)

        def st0(bk, ii, q=None):
            cs = part(q, 512)
            nc.sync.dma_start(out=o0v[rows(bk, ii), cs], in_=osb[(bk, ii)][:, cs])

        def amax_(bk, ii, q=None):
            if (bk, ii) not in ams:
                ams[(bk, ii)] = small.tile([P, H], F32, name="amax", tag="amax")
                rin[(bk, ii)] = small.tile([P, H], F32, name="rinv", tag="rinv")
                facs[(bk, ii)] = small.tile([P, H], F32, name="fac", tag="fac")
                f8s[(bk, ii)] = op.tile([P, D], FP8, name="f8", tag="f8")
            nc.vector.tensor_reduce(
                out=ams[(bk, ii)][:, part(q, 4)],
                in_=osb[(bk, ii)][:, part(q, 512)].rearrange("p (h c) -> p h c", c=HD),
                axis=AX.X,
                op=ALU.max,
                apply_absolute_value=True,
            )

        def rinv_(bk, ii, q=None):
            hs = part(q, 4)
            nc.vector.reciprocal(out=rin[(bk, ii)][:, hs], in_=ams[(bk, ii)][:, hs])

        def fac_(bk, ii, q=None):
            hs = part(q, 4)
            nc.vector.tensor_scalar(
                out=facs[(bk, ii)][:, hs], in0=rin[(bk, ii)][:, hs], scalar1=448.0, scalar2=None, op0=ALU.mult
            )

        def cast(bk, ii, h, on_vector):
            cs = slice(h * HD, (h + 1) * HD)
            o_sb, fac, f8 = osb[(bk, ii)], facs[(bk, ii)], f8s[(bk, ii)]
            if on_vector:
                nc.vector.tensor_scalar(
                    out=f8[:, cs], in0=o_sb[:, cs], scalar1=fac[:, h : h + 1], scalar2=None, op0=ALU.mult, saturate=False
                )
            else:
                nc.scalar.activation(
                    out=f8[:, cs],
                    in_=o_sb[:, cs],
                    func=ACT.Identity,
                    scale=fac[:, h : h + 1],
                    bias=zeros[:, 0:1],
                    saturate=False,
                )

        def st1(bk, ii, q=None):
            cs = part(q, 512)
            nc.sync.dma_start(out=o1v[rows(bk, ii), cs], in_=f8s[(bk, ii)][:, cs].bitcast(U8))

        def ok(bk):
            return 0 <= bk < NBLK

        def castV(bk, ii, heads):
            for h in heads:
                cast(bk, ii, h, True)

        def castS(bk, ii, heads):
            for h in heads:
                cast(bk, ii, h, False)

        load_cs()
        consts()
        load_w(0)
        load_w(1)
        load_x(0)
        load_x(1)
        load_w(2)
        load_bg()
        for n in (3, 4, 5, 6):
            load_w(n)
        load_x(2)
        load_x(3)
        load_w(7)
        load_x(4)
        load_x(5)
        load_w(8)
        load_x(6)
        load_x(7)

        sgn_T()
        dup(0)
        dup(1)
        sgn_cp()
        w_il(0)
        w_il(1)
        w_q(0)
        w_q(1)
        for s, half in EARLY:
            rot_T(s, half)
        x_T(0)
        for k in range(KP):
            x_cp(0, k)
        w_il(2)
        for k in range(KP):
            x_q(0, k)
        w_q(2)
        w_il(3)
        for s in range(2):
            for half in range(2):
                if (s, half) not in EARLY:
                    rot_T(s, half)
                rot_cp(s, half)
        w_il(4)
        bgf()
        cols_T()
        cols_cp()
        w_il(5)
        w_q(3)

        for p in range(NBLK + 1):
            a, bb, cc = p, p - 1, p - 2
            if ok(a):
                for h in (0, 1, 2, 3):
                    mx_(a, h)
            if ok(bb):
                sq_T(bb)
            if p >= 2 and ok(a + 1):
                x_T(a + 1)
            if ok(a):
                for h in (0, 1, 2, 3):
                    usq(a, h)
            if ok(cc) and cc < LAST:
                castS(cc, 0, [h for h in range(H) if h not in VHB[cc]])
            if p == 0:
                w_q(5)
                w_q(4)
                w_il(7)
                w_il(6)
            if ok(a):
                for h in (0, 1, 2, 3):
                    yy(a, h)
            if ok(cc) and cc < LAST:
                castV(cc, 0, VHB[cc][4:])
                st1(cc, 0)
            if ok(bb):
                red(bb)
            if ok(cc) and cc < LAST:
                amax_(cc, 1)
            if p >= 1 and ok(a + 1):
                for k in range(KP):
                    x_cp(a + 1, k)
            if ok(bb):
                ars(bb)
            if p >= 1 and ok(a + 1):
                x_q(a + 1, 0)
                x_q(a + 1, 1)
            if ok(cc) and cc < LAST and ok(a + 1):
                rinv_(cc, 1)
            if p >= 1 and ok(a + 1):
                x_q(a + 1, 2)
            if ok(a):
                for h in (4, 5, 6, 7):
                    mx_(a, h)
            if p == 0:
                x_T(1)
                x_T(2)
            if ok(bb):
                for q in range(3):
                    o_T(bb, 0, q)
            if p == 0:
                for k in range(KP):
                    x_cp(1, k)
            if ok(a):
                for h in (4, 5, 6, 7):
                    usq(a, h)
            if p == 0:
                w_il(8)
                w_q(6)
                w_q(7)
                w_q(8)
            if ok(bb) and bb < LAST:
                for q in range(3):
                    evac(bb, 0, q)
                st0(bb, 0)
            if bb == LAST:
                for q in range(3):
                    evac(bb, 0, q)
                    st0(bb, 0, q)
            if p == 0:
                for k in range(KP):
                    x_q(1, k)
            if ok(a):
                yy(a, 4)
            if ok(cc) and cc < LAST and ok(a) and not ok(a + 1):
                rinv_(cc, 1)
            if ok(a):
                yy(a, 5)
            if ok(cc) and cc < LAST and ok(a):
                fac_(cc, 1)
            if ok(a):
                yy(a, 6)
                yy(a, 7)
            if ok(cc) and cc < LAST and ok(a):
                castV(cc, 1, VHB[cc])
                castS(cc, 1, [h for h in range(H) if h not in VHB[cc]])
                st1(cc, 1)
            if ok(bb) and bb < LAST:
                amax_(bb, 0)
            if ok(a):
                for h in (8, 9, 10, 11):
                    mx_(a, h)
            if ok(bb):
                for q in range(3):
                    o_T(bb, 1, q)
            if ok(a):
                for h in (8, 9, 10, 11):
                    usq(a, h)
            if ok(bb) and bb < LAST:
                for q in range(3):
                    evac(bb, 1, q)
                st0(bb, 1)
            if ok(a):
                yy(a, 8)
            if ok(bb) and bb < LAST:
                rinv_(bb, 0)
            if ok(a):
                yy(a, 9)
            if ok(bb) and bb < LAST:
                fac_(bb, 0)
            if ok(a):
                yy(a, 10)
                yy(a, 11)
            if ok(bb) and bb < LAST:
                castV(bb, 0, VHB[bb][:4])
            if bb == LAST:
                for q in range(3):
                    evac(bb, 1, q)
                    st0(bb, 1, q)
                units = [(cc, 1, None)] + [(bb, ii, q) for ii in range(TPB) for q in range(3)]
                for n in range(len(units) + 3):
                    if 1 <= n < len(units):
                        amax_(*units[n])
                    if 0 <= n - 1 < len(units):
                        rinv_(*units[n - 1])
                    if 0 <= n - 2 < len(units):
                        fac_(*units[n - 2])
                    if 0 <= n - 3 < len(units):
                        bk, ii, q = units[n - 3]
                        heads = range(H) if q is None else range(4 * q, 4 * q + 4)
                        castV(bk, ii, [h for h in heads if h in (VHB[bk] if q is None else VL)])
                        castS(bk, ii, [h for h in heads if h not in (VHB[bk] if q is None else VL)])
                        st1(bk, ii, q)
